import numpy as np
import ml_dtypes


def mxq(x, axis, fmt="e4m3"):
    dtype, down = {"e4m3": (ml_dtypes.float8_e4m3fn, 7), "e5m2": (ml_dtypes.float8_e5m2, 14)}[fmt]
    v = np.moveaxis(np.asarray(x, np.float32).astype(ml_dtypes.bfloat16).astype(np.float64), axis, -1)
    blocks = v.reshape(v.shape[:-1] + (-1, 32))
    amax = np.abs(blocks).max(-1, keepdims=True)
    byte = np.maximum(np.where(amax > 0, np.frexp(amax)[1] - 1 + 127, 0) - down, 1)
    scale = np.exp2(byte - 127.0)
    codes = (blocks / scale).astype(np.float32).astype(dtype).astype(np.float64)
    return np.moveaxis((codes * scale).reshape(v.shape), -1, axis)


WIDE = False


def mx_kscale(k):
    if not WIDE:
        return np.ones(k)
    levels = np.array([10, -10, 5, -5, 0])
    if k % 512:
        return np.exp2(np.random.permutation(np.resize(levels, k // 32))).repeat(32)
    a = np.empty((k // 512, 16))
    for p in range(k // 512):
        a[p, :8] = np.random.permutation(np.resize(levels, 8))
        for g in range(8):
            far = levels[np.abs(levels - a[p, g]) >= 10]
            a[p, g + 8] = far[np.random.randint(len(far))]
    return np.exp2(a.ravel()).repeat(32)


BF16 = ml_dtypes.bfloat16


def bf(x):
    return np.asarray(x, np.float32).astype(BF16)


def f64(x):
    return np.asarray(x).astype(np.float64)


B, DIN, H1, H2, N, I, K, O = 4096, 2048, 1024, 512, 64, 16, 64, 16
NI = N * I
KO = K * O
SQ_EPS = 1e-8


def squash(t):
    sq = np.sum(t * t, axis=-1, keepdims=True)
    return (sq / (1.0 + sq)) * t / np.sqrt(sq + SQ_EPS)


def setup_inputs():
    s = mx_kscale(NI).reshape(N, I)
    return {"p": bf(np.random.standard_normal((B, N, I)) * s),
            "Wr": bf(np.random.standard_normal((N, K, O, I)) * K / np.sqrt(NI * O) / s[:, None, None, :])}


def reference(p, Wr):
    c = 1.0 / K
    pf = f64(p).reshape(B, NI)
    wf = f64(Wr).transpose(0, 3, 1, 2).reshape(NI, KO)
    s = (mxq(pf, 1, "e4m3") @ mxq(wf, 0, "e4m3")).reshape(B, K, O) * c
    return squash(s)

@@ -1,0 +1,258 @@
+from contextlib import ExitStack
+
+import concourse.mybir as mybir
+from concourse.masks import make_identity
+
+F32 = mybir.dt.float32
+BF16 = mybir.dt.bfloat16
+U32 = mybir.dt.uint32
+U8 = mybir.dt.uint8
+FP8X4 = mybir.dt.float8_e4m3fn_x4
+ACT = mybir.ActivationFunctionType
+ALU = mybir.AluOpType
+
+P = 128
+BATCH = 4096
+CAPS_IN = 64
+DIM_IN = 16
+CAPS_OUT = 64
+DIM_OUT = 16
+K = CAPS_IN * DIM_IN
+COLS = CAPS_OUT * DIM_OUT
+PACK = 4
+K_PASS = P * PACK
+PASSES = K // K_PASS
+PLANES = 2
+CAPS_PLANE = CAPS_IN // (PASSES * PLANES)
+WORDS_IN = DIM_IN // 2
+COLS_PART = COLS // P
+BANK = 512
+HALVES = COLS // BANK
+CAPS_BANK = BANK // DIM_OUT
+TILES = BATCH // P
+LOAD_TILES = 4
+COUPLING = 1.0 / CAPS_OUT
+SQ_EPS = 1e-8
+
+AHEAD_NORM = 1
+AHEAD_MULTIPLY = 3
+AHEAD_QUANTISE = 5
+AHEAD_TRANSPOSE = 7
+
+FLOPS = 2 * BATCH * K * COLS
+
+
+def tile_capsulenetwork_pb_t_kernel(tc, p, Wr, out):
+    nc = tc.nc
+    p_view = p.rearrange("(row t) n i -> row t (n i)", t=TILES)
+    out_view = out.rearrange("(row t) j o -> row t (j o)", t=TILES)
+    w_view = Wr.rearrange("n j (oh ol) i -> (j oh) n (ol i)", ol=COLS_PART)
+
+    with ExitStack() as ctx:
+        const = ctx.enter_context(tc.tile_pool(name="const", bufs=1))
+        weights = ctx.enter_context(tc.tile_pool(name="weights", bufs=1))
+        rows = ctx.enter_context(tc.tile_pool(name="rows", bufs=1))
+        work = ctx.enter_context(tc.tile_pool(name="work", bufs=4))
+        psum = ctx.enter_context(tc.psum_pool(name="psum", bufs=8))
+        ctx.enter_context(tc.manual_schedule())
+
+        w_raw = weights.tile([P, CAPS_IN, COLS_PART * DIM_IN], BF16)
+        for plane in range(PASSES * PLANES):
+            caps = slice(plane * CAPS_PLANE, (plane + 1) * CAPS_PLANE)
+            nc.sync.dma_start(out=w_raw[:, caps, :], in_=w_view[:, caps, :])
+        p_rows = []
+        for c in range(TILES // LOAD_TILES):
+            chunk = rows.tile([P, LOAD_TILES, K], BF16, name="p_rows%d" % c)
+            nc.sync.dma_start(out=chunk[:], in_=p_view[:, c * LOAD_TILES : (c + 1) * LOAD_TILES, :])
+            p_rows.append(chunk)
+
+        ident = const.tile([P, P], F32)
+        make_identity(nc, ident[:])
+        eps_bias = const.tile([P, 1], F32)
+        nc.vector.memset(eps_bias[:], SQ_EPS / (COUPLING * COUPLING))
+        one_bias = const.tile([P, 1], F32)
+        nc.vector.memset(one_bias[:], 1.0)
+        table_warm = const.tile([P, 1], F32)
+        nc.scalar.activation(out=table_warm[:], in_=one_bias[:], func=ACT.Abs_reciprocal_sqrt)
+
+        w_raw_words = w_raw[:].bitcast(F32).rearrange("c n (ol w) -> c ol n w", ol=COLS_PART)
+        w_sorted = weights.tile([P, PASSES, COLS_PART, PLANES, P], F32)
+        w_grouped = weights.tile([P, PASSES, COLS * PACK], BF16, align_bytes=64)
+        w_grouped_words = w_grouped[:].bitcast(F32).rearrange(
+            "r g (c ol u) -> r g c ol u", ol=COLS_PART, u=PLANES
+        )
+        w_codes = weights.tile([P, PASSES, COLS], U32, align_bytes=64)
+        w_scales = weights.tile([P, PASSES, COLS], U8, align_bytes=64)
+        OL_BANK = 2
+
+        def quantise_weights(g):
+            nc.vector.quantize_mx(
+                out=w_codes[:, g, :].bitcast(FP8X4), scales=w_scales[:, g, :], in_=w_grouped[:, g, :]
+            )
+
+        for g in range(PASSES):
+            w_banks = []
+            for u in range(PLANES):
+                plane = g * PLANES + u
+                caps = slice(plane * CAPS_PLANE, (plane + 1) * CAPS_PLANE)
+                for m in range(COLS_PART // OL_BANK):
+                    ols = slice(m * OL_BANK, (m + 1) * OL_BANK)
+                    nc.vector.tensor_copy(
+                        out=w_sorted[:, g, ols, u, :].rearrange("c ol (n w) -> c ol n w", w=WORDS_IN),
+                        in_=w_raw_words[:, ols, caps, :],
+                    )
+            for m in range(COLS_PART // OL_BANK):
+                w_banks.append(psum.tile([P, OL_BANK, PLANES, P], F32, name="w_bank", tag="bank"))
+                for a in range(OL_BANK):
+                    words = w_sorted[:, g, m * OL_BANK + a, :, :].rearrange("c h w -> c (h w)")
+                    for u in range(PLANES):
+                        nc.tensor.transpose(w_banks[m][:, a, u, :], words[:, u::PLANES], ident[:])
+            if g > 0:
+                quantise_weights(g - 1)
+            for m in range(COLS_PART // OL_BANK):
+                copy = nc.scalar.copy if m < 2 else nc.vector.tensor_copy
+                copy(
+                    out=w_grouped_words[:, g, :, m * OL_BANK : (m + 1) * OL_BANK, :],
+                    in_=w_banks[m][:].rearrange("r a u c -> r c a u"),
+                )
+        quantise_weights(PASSES - 1)
+
+        flipped = {}
+        grouped = {}
+        codes = {}
+        scales = {}
+        banks = {}
+        squares = {}
+        folded = {}
+        lengths = {}
+        inv_roots = {}
+        inv_1q = {}
+        units = {}
+        factors = {}
+        squashed = {}
+
+        def transpose_rows(t):
+            words = p_rows[t // LOAD_TILES][:, t % LOAD_TILES, :].bitcast(F32)
+            flipped[t] = psum.tile([P, PASSES * PLANES, P], F32, name="flipped", tag="bank")
+            for x in range(PASSES * PLANES):
+                nc.tensor.transpose(flipped[t][:, x, :], words[:, (x // PLANES) * PLANES * P + x % PLANES : (x // PLANES + 1) * PLANES * P : PLANES], ident[:])
+
+        def group_rows(t):
+            grouped[t] = work.tile([P, PASSES, P * PACK], BF16, name="grouped", align_bytes=64)
+            nc.scalar.copy(
+                out=grouped[t][:].bitcast(F32).rearrange("r g (row u) -> r g row u", u=PLANES),
+                in_=flipped[t][:].rearrange("r (g u) row -> r g row u", u=PLANES),
+            )
+
+        def quantise_rows(t):
+            codes[t] = work.tile([P, PASSES, P], U32, name="codes", align_bytes=64)
+            scales[t] = work.tile([P, PASSES, P], U8, name="scales", align_bytes=64)
+            nc.vector.quantize_mx(
+                out=codes[t][:].rearrange("r g row -> r (g row)").bitcast(FP8X4),
+                scales=scales[t][:].rearrange("r g row -> r (g row)"),
+                in_=grouped[t][:].rearrange("r g c -> r (g c)"),
+            )
+
+        def multiply(t, h):
+            cols = slice(h * BANK, (h + 1) * BANK)
+            bank = psum.tile([P, BANK], F32, tag="bank")
+            for g in range(PASSES):
+                nc.tensor.matmul_mx(
+                    out=bank[:],
+                    lhsT=codes[t][:, g, :].bitcast(FP8X4),
+                    lhsT_scale=scales[t][:, g, :],
+                    rhs=w_codes[:, g, cols].bitcast(FP8X4),
+                    rhs_scale=w_scales[:, g, cols],
+                    start=(g == 0),
+                    stop=(g == PASSES - 1),
+                )
+            banks[t, h] = bank
+
+        def square(t, h):
+            if h == 0:
+                squares[t] = work.tile([P, COLS], F32, name="squares")
+                folded[t] = work.tile([P, COLS // 2], F32, name="folded")
+            nc.scalar.activation(
+                out=squares[t][:, h * BANK : (h + 1) * BANK], in_=banks[t, h][:], func=ACT.Square, scale=COUPLING
+            )
+            pairs = squares[t][:, h * BANK : (h + 1) * BANK].rearrange("row (j o) -> row j o", o=DIM_OUT)
+            nc.gpsimd.tensor_tensor(
+                out=folded[t][:, h * BANK // 2 : (h + 1) * BANK // 2].rearrange("row (j o) -> row j o", o=DIM_OUT // 2),
+                in0=pairs[:, :, 0 : DIM_OUT // 2],
+                in1=pairs[:, :, DIM_OUT // 2 : DIM_OUT],
+                op=ALU.add,
+            )
+
+        def length(t):
+            lengths[t] = work.tile([P, CAPS_OUT], F32, name="lengths")
+            nc.vector.tensor_reduce(
+                out=lengths[t][:],
+                in_=folded[t][:].rearrange("row (j o) -> row j o", j=CAPS_OUT),
+                axis=mybir.AxisListType.X,
+                op=ALU.add,
+            )
+            inv_sqrt_1q = work.tile([P, CAPS_OUT], F32, name="inv_sqrt_1q")
+            inv_roots[t] = work.tile([P, CAPS_OUT], F32, name="inv_roots")
+            inv_1q[t] = work.tile([P, CAPS_OUT], F32, name="inv_1q")
+            nc.scalar.activation(
+                out=inv_sqrt_1q[:], in_=lengths[t][:], func=ACT.Abs_reciprocal_sqrt, bias=one_bias[:]
+            )
+            nc.scalar.activation(
+                out=inv_roots[t][:],
+                in_=lengths[t][:],
+                func=ACT.Abs_reciprocal_sqrt,
+                bias=eps_bias[:],
+                scale=1.0 / (COUPLING * COUPLING),
+            )
+            nc.scalar.activation(out=inv_1q[t][:], in_=inv_sqrt_1q[:], func=ACT.Square)
+
+        def unit(t):
+            units[t] = work.tile([P, CAPS_OUT], F32, name="units")
+            nc.vector.tensor_tensor(out=units[t][:], in0=lengths[t][:], in1=inv_roots[t][:], op=ALU.mult)
+
+        def factor(t):
+            factors[t] = work.tile([P, CAPS_OUT], F32, name="factors")
+            nc.vector.tensor_tensor(out=factors[t][:], in0=units[t][:], in1=inv_1q[t][:], op=ALU.mult)
+
+        def scale_half(t, h):
+            if h == 0:
+                squashed[t] = work.tile([P, COLS], F32, name="squashed")
+            nc.vector.tensor_tensor(
+                out=squashed[t][:, h * BANK : (h + 1) * BANK].rearrange("row (j o) -> row j o", o=DIM_OUT),
+                in0=banks[t, h][:].rearrange("row (j o) -> row j o", o=DIM_OUT),
+                in1=factors[t][:, h * CAPS_BANK : (h + 1) * CAPS_BANK]
+                .unsqueeze(2)
+                .to_broadcast([P, CAPS_BANK, DIM_OUT]),
+                op=ALU.mult,
+            )
+
+        def store(t):
+            nc.sync.dma_start(out=out_view[:, t, :], in_=squashed[t][:])
+
+        def live(t):
+            return 0 <= t < TILES
+
+        for s in range(-AHEAD_TRANSPOSE, TILES):
+            if live(s + AHEAD_NORM):
+                length(s + AHEAD_NORM)
+            if live(s + AHEAD_QUANTISE):
+                quantise_rows(s + AHEAD_QUANTISE)
+            if live(s):
+                scale_half(s, 0)
+            if live(s + AHEAD_NORM):
+                unit(s + AHEAD_NORM)
+            if live(s):
+                scale_half(s, 1)
+                store(s)
+            if live(s + AHEAD_NORM):
+                factor(s + AHEAD_NORM)
+            if live(s + AHEAD_TRANSPOSE):
+                transpose_rows(s + AHEAD_TRANSPOSE)
+            if live(s + AHEAD_MULTIPLY):
+                multiply(s + AHEAD_MULTIPLY, 0)
+                square(s + AHEAD_MULTIPLY, 0)
+            if live(s + AHEAD_TRANSPOSE):
+                group_rows(s + AHEAD_TRANSPOSE)
+            if live(s + AHEAD_MULTIPLY):
+                multiply(s + AHEAD_MULTIPLY, 1)
+                square(s + AHEAD_MULTIPLY, 1)

@@ -28,13 +28,16 @@ WORDS_IN = DIM_IN // 2
 COLS_PART = COLS // P
 BANK = 512
 HALVES = COLS // BANK
-CAPS_BANK = BANK // DIM_OUT
+OL_BANK = 2
+OL_HALF = COLS_PART // HALVES
+OH = DIM_OUT // COLS_PART
 TILES = BATCH // P
-LOAD_TILES = 4
+LOAD_WIDTHS = [1, 1, 2] + [4] * 7
 COUPLING = 1.0 / CAPS_OUT
 SQ_EPS = 1e-8
 
 AHEAD_NORM = 1
+AHEAD_FOLD = 2
 AHEAD_MULTIPLY = 3
 AHEAD_QUANTISE = 5
 AHEAD_TRANSPOSE = 7
@@ -53,6 +56,7 @@ def tile_capsulenetwork_pb_t_kernel(tc, p, Wr, out):
         weights = ctx.enter_context(tc.tile_pool(name="weights", bufs=1))
         rows = ctx.enter_context(tc.tile_pool(name="rows", bufs=1))
         work = ctx.enter_context(tc.tile_pool(name="work", bufs=4))
+        sums = ctx.enter_context(tc.tile_pool(name="sums", bufs=2))
         psum = ctx.enter_context(tc.psum_pool(name="psum", bufs=8))
         ctx.enter_context(tc.manual_schedule())
 
@@ -60,11 +64,14 @@ def tile_capsulenetwork_pb_t_kernel(tc, p, Wr, out):
         for plane in range(PASSES * PLANES):
             caps = slice(plane * CAPS_PLANE, (plane + 1) * CAPS_PLANE)
             nc.sync.dma_start(out=w_raw[:, caps, :], in_=w_view[:, caps, :])
-        p_rows = []
-        for c in range(TILES // LOAD_TILES):
-            chunk = rows.tile([P, LOAD_TILES, K], BF16, name="p_rows%d" % c)
-            nc.sync.dma_start(out=chunk[:], in_=p_view[:, c * LOAD_TILES : (c + 1) * LOAD_TILES, :])
-            p_rows.append(chunk)
+        p_rows = {}
+        first = 0
+        for c, width in enumerate(LOAD_WIDTHS):
+            chunk = rows.tile([P, width, K], BF16, name="p_rows%d" % c)
+            nc.sync.dma_start(out=chunk[:], in_=p_view[:, first : first + width, :])
+            for x in range(width):
+                p_rows[first + x] = chunk[:, x, :]
+            first += width
 
         ident = const.tile([P, P], F32)
         make_identity(nc, ident[:])
@@ -78,44 +85,50 @@ def tile_capsulenetwork_pb_t_kernel(tc, p, Wr, out):
         w_raw_words = w_raw[:].bitcast(F32).rearrange("c n (ol w) -> c ol n w", ol=COLS_PART)
         w_sorted = weights.tile([P, PASSES, COLS_PART, PLANES, P], F32)
         w_grouped = weights.tile([P, PASSES, COLS * PACK], BF16, align_bytes=64)
-        w_grouped_words = w_grouped[:].bitcast(F32).rearrange(
-            "r g (c ol u) -> r g c ol u", ol=COLS_PART, u=PLANES
-        )
+        w_grouped_words = w_grouped[:].bitcast(F32).rearrange("r g (ol c u) -> r g ol c u", ol=COLS_PART, u=PLANES)
         w_codes = weights.tile([P, PASSES, COLS], U32, align_bytes=64)
         w_scales = weights.tile([P, PASSES, COLS], U8, align_bytes=64)
-        OL_BANK = 2
 
-        def quantise_weights(g):
-            nc.vector.quantize_mx(
-                out=w_codes[:, g, :].bitcast(FP8X4), scales=w_scales[:, g, :], in_=w_grouped[:, g, :]
-            )
-
-        for g in range(PASSES):
-            w_banks = []
-            for u in range(PLANES):
-                plane = g * PLANES + u
-                caps = slice(plane * CAPS_PLANE, (plane + 1) * CAPS_PLANE)
-                for m in range(COLS_PART // OL_BANK):
-                    ols = slice(m * OL_BANK, (m + 1) * OL_BANK)
-                    nc.vector.tensor_copy(
-                        out=w_sorted[:, g, ols, u, :].rearrange("c ol (n w) -> c ol n w", w=WORDS_IN),
-                        in_=w_raw_words[:, ols, caps, :],
-                    )
+        def sort_weights(plane):
+            g, q = divmod(plane, PLANES)
+            caps = slice(plane * CAPS_PLANE, (plane + 1) * CAPS_PLANE)
             for m in range(COLS_PART // OL_BANK):
-                w_banks.append(psum.tile([P, OL_BANK, PLANES, P], F32, name="w_bank", tag="bank"))
+                ols = slice(m * OL_BANK, (m + 1) * OL_BANK)
+                nc.vector.tensor_copy(
+                    out=w_sorted[:, g, ols, q, :].rearrange("c ol (n w) -> c ol n w", w=WORDS_IN),
+                    in_=w_raw_words[:, ols, caps, :],
+                )
+
+        def transpose_weights(g):
+            for m in range(COLS_PART // OL_BANK):
+                w_bank = psum.tile([P, OL_BANK, PLANES, P], F32, name="w_bank", tag="bank")
                 for a in range(OL_BANK):
                     words = w_sorted[:, g, m * OL_BANK + a, :, :].rearrange("c h w -> c (h w)")
                     for u in range(PLANES):
-                        nc.tensor.transpose(w_banks[m][:, a, u, :], words[:, u::PLANES], ident[:])
-            if g > 0:
-                quantise_weights(g - 1)
-            for m in range(COLS_PART // OL_BANK):
-                copy = nc.scalar.copy if m < 2 else nc.vector.tensor_copy
-                copy(
-                    out=w_grouped_words[:, g, :, m * OL_BANK : (m + 1) * OL_BANK, :],
-                    in_=w_banks[m][:].rearrange("r a u c -> r c a u"),
+                        nc.tensor.transpose(w_bank[:, a, u, :], words[:, u::PLANES], ident[:])
+                nc.scalar.copy(
+                    out=w_grouped_words[:, g, m * OL_BANK : (m + 1) * OL_BANK, :, :],
+                    in_=w_bank[:].rearrange("r a u c -> r a c u"),
                 )
-        quantise_weights(PASSES - 1)
+
+        def quantise_weights(g):
+            width = OL_BANK * P
+            for m in range(COLS_PART // OL_BANK):
+                cols = slice(m * width, (m + 1) * width)
+                nc.vector.quantize_mx(
+                    out=w_codes[:, g, cols].bitcast(FP8X4),
+                    scales=w_scales[:, g, cols],
+                    in_=w_grouped[:, g, m * width * PACK : (m + 1) * width * PACK],
+                )
+
+        sort_weights(0)
+        sort_weights(1)
+        transpose_weights(0)
+        sort_weights(2)
+        quantise_weights(0)
+        sort_weights(3)
+        transpose_weights(1)
+        quantise_weights(1)
 
         flipped = {}
         grouped = {}
@@ -127,12 +140,11 @@ def tile_capsulenetwork_pb_t_kernel(tc, p, Wr, out):
         lengths = {}
         inv_roots = {}
         inv_1q = {}
-        units = {}
         factors = {}
         squashed = {}
 
         def transpose_rows(t):
-            words = p_rows[t // LOAD_TILES][:, t % LOAD_TILES, :].bitcast(F32)
+            words = p_rows[t].bitcast(F32)
             flipped[t] = psum.tile([P, PASSES * PLANES, P], F32, name="flipped", tag="bank")
             for x in range(PASSES * PLANES):
                 nc.tensor.transpose(flipped[t][:, x, :], words[:, (x // PLANES) * PLANES * P + x % PLANES : (x // PLANES + 1) * PLANES * P : PLANES], ident[:])
@@ -171,26 +183,36 @@ def tile_capsulenetwork_pb_t_kernel(tc, p, Wr, out):
         def square(t, h):
             if h == 0:
                 squares[t] = work.tile([P, COLS], F32, name="squares")
-                folded[t] = work.tile([P, COLS // 2], F32, name="folded")
             nc.scalar.activation(
-                out=squares[t][:, h * BANK : (h + 1) * BANK], in_=banks[t, h][:], func=ACT.Square, scale=COUPLING
+                out=squares[t][:, h * BANK : (h + 1) * BANK].rearrange("row (c ol) -> row c ol", ol=OL_HALF),
+                in_=banks[t, h][:].rearrange("row (ol c) -> row c ol", ol=OL_HALF),
+                func=ACT.Square,
+                scale=COUPLING,
             )
-            pairs = squares[t][:, h * BANK : (h + 1) * BANK].rearrange("row (j o) -> row j o", o=DIM_OUT)
-            nc.gpsimd.tensor_tensor(
-                out=folded[t][:, h * BANK // 2 : (h + 1) * BANK // 2].rearrange("row (j o) -> row j o", o=DIM_OUT // 2),
-                in0=pairs[:, :, 0 : DIM_OUT // 2],
-                in1=pairs[:, :, DIM_OUT // 2 : DIM_OUT],
-                op=ALU.add,
-            )
+
+        def fold(t):
+            folded[t] = sums.tile([P, COLS // 2 + CAPS_OUT], F32, name="folded")
+            for h in range(HALVES):
+                pairs = squares[t][:, h * BANK : (h + 1) * BANK].rearrange(
+                    "row (j oh ol) -> row j oh ol", oh=OH, ol=OL_HALF
+                )
+                nc.gpsimd.tensor_tensor(
+                    out=folded[t][:, : COLS // 2].rearrange("row (j h ol) -> row h j ol", h=HALVES, ol=OL_HALF)[:, h],
+                    in0=pairs[:, :, 0, :],
+                    in1=pairs[:, :, 1, :],
+                    op=ALU.add,
+                )
 
         def length(t):
             lengths[t] = work.tile([P, CAPS_OUT], F32, name="lengths")
             nc.vector.tensor_reduce(
                 out=lengths[t][:],
-                in_=folded[t][:].rearrange("row (j o) -> row j o", j=CAPS_OUT),
+                in_=folded[t][:, : COLS // 2].rearrange("row (j o) -> row j o", j=CAPS_OUT),
                 axis=mybir.AxisListType.X,
                 op=ALU.add,
             )
+
+        def roots(t):
             inv_sqrt_1q = work.tile([P, CAPS_OUT], F32, name="inv_sqrt_1q")
             inv_roots[t] = work.tile([P, CAPS_OUT], F32, name="inv_roots")
             inv_1q[t] = work.tile([P, CAPS_OUT], F32, name="inv_1q")
@@ -207,22 +229,21 @@ def tile_capsulenetwork_pb_t_kernel(tc, p, Wr, out):
             nc.scalar.activation(out=inv_1q[t][:], in_=inv_sqrt_1q[:], func=ACT.Square)
 
         def unit(t):
-            units[t] = work.tile([P, CAPS_OUT], F32, name="units")
-            nc.vector.tensor_tensor(out=units[t][:], in0=lengths[t][:], in1=inv_roots[t][:], op=ALU.mult)
+            nc.vector.tensor_tensor(
+                out=folded[t][:, COLS // 2 :], in0=lengths[t][:], in1=inv_roots[t][:], op=ALU.mult
+            )
 
         def factor(t):
             factors[t] = work.tile([P, CAPS_OUT], F32, name="factors")
-            nc.vector.tensor_tensor(out=factors[t][:], in0=units[t][:], in1=inv_1q[t][:], op=ALU.mult)
+            nc.vector.tensor_tensor(out=factors[t][:], in0=folded[t][:, COLS // 2 :], in1=inv_1q[t][:], op=ALU.mult)
 
         def scale_half(t, h):
             if h == 0:
                 squashed[t] = work.tile([P, COLS], F32, name="squashed")
             nc.vector.tensor_tensor(
-                out=squashed[t][:, h * BANK : (h + 1) * BANK].rearrange("row (j o) -> row j o", o=DIM_OUT),
-                in0=banks[t, h][:].rearrange("row (j o) -> row j o", o=DIM_OUT),
-                in1=factors[t][:, h * CAPS_BANK : (h + 1) * CAPS_BANK]
-                .unsqueeze(2)
-                .to_broadcast([P, CAPS_BANK, DIM_OUT]),
+                out=squashed[t][:].rearrange("row (j oh h ol) -> row h j oh ol", oh=OH, h=HALVES, ol=OL_HALF)[:, h],
+                in0=banks[t, h][:].rearrange("row (ol j oh) -> row j oh ol", ol=OL_HALF, oh=OH),
+                in1=factors[t][:].unsqueeze(2).unsqueeze(3).to_broadcast([P, CAPS_OUT, OH, OL_HALF]),
                 op=ALU.mult,
             )
 
@@ -233,26 +254,27 @@ def tile_capsulenetwork_pb_t_kernel(tc, p, Wr, out):
             return 0 <= t < TILES
 
         for s in range(-AHEAD_TRANSPOSE, TILES):
-            if live(s + AHEAD_NORM):
-                length(s + AHEAD_NORM)
+            if live(s + AHEAD_TRANSPOSE):
+                transpose_rows(s + AHEAD_TRANSPOSE)
+                group_rows(s + AHEAD_TRANSPOSE)
+            if live(s + AHEAD_MULTIPLY):
+                multiply(s + AHEAD_MULTIPLY, 0)
+            if live(s):
+                unit(s)
             if live(s + AHEAD_QUANTISE):
                 quantise_rows(s + AHEAD_QUANTISE)
             if live(s):
-                scale_half(s, 0)
+                factor(s)
+            if live(s + AHEAD_FOLD):
+                fold(s + AHEAD_FOLD)
             if live(s + AHEAD_NORM):
-                unit(s + AHEAD_NORM)
-            if live(s):
-                scale_half(s, 1)
-                store(s)
-            if live(s + AHEAD_NORM):
-                factor(s + AHEAD_NORM)
-            if live(s + AHEAD_TRANSPOSE):
-                transpose_rows(s + AHEAD_TRANSPOSE)
+                length(s + AHEAD_NORM)
+                roots(s + AHEAD_NORM)
             if live(s + AHEAD_MULTIPLY):
-                multiply(s + AHEAD_MULTIPLY, 0)
                 square(s + AHEAD_MULTIPLY, 0)
-            if live(s + AHEAD_TRANSPOSE):
-                group_rows(s + AHEAD_TRANSPOSE)
-            if live(s + AHEAD_MULTIPLY):
                 multiply(s + AHEAD_MULTIPLY, 1)
                 square(s + AHEAD_MULTIPLY, 1)
+            if live(s):
+                scale_half(s, 0)
+                scale_half(s, 1)
+                store(s)

@@ -139,6 +139,7 @@ def tile_capsulenetwork_pb_t_kernel(tc, p, Wr, out):
         folded = {}
         lengths = {}
         inv_roots = {}
+        inv_sqrt_1q = {}
         inv_1q = {}
         factors = {}
         squashed = {}
@@ -213,12 +214,8 @@ def tile_capsulenetwork_pb_t_kernel(tc, p, Wr, out):
             )
 
         def roots(t):
-            inv_sqrt_1q = work.tile([P, CAPS_OUT], F32, name="inv_sqrt_1q")
             inv_roots[t] = work.tile([P, CAPS_OUT], F32, name="inv_roots")
-            inv_1q[t] = work.tile([P, CAPS_OUT], F32, name="inv_1q")
-            nc.scalar.activation(
-                out=inv_sqrt_1q[:], in_=lengths[t][:], func=ACT.Abs_reciprocal_sqrt, bias=one_bias[:]
-            )
+            inv_sqrt_1q[t] = work.tile([P, CAPS_OUT], F32, name="inv_sqrt_1q")
             nc.scalar.activation(
                 out=inv_roots[t][:],
                 in_=lengths[t][:],
@@ -226,7 +223,13 @@ def tile_capsulenetwork_pb_t_kernel(tc, p, Wr, out):
                 bias=eps_bias[:],
                 scale=1.0 / (COUPLING * COUPLING),
             )
-            nc.scalar.activation(out=inv_1q[t][:], in_=inv_sqrt_1q[:], func=ACT.Square)
+            nc.scalar.activation(
+                out=inv_sqrt_1q[t][:], in_=lengths[t][:], func=ACT.Abs_reciprocal_sqrt, bias=one_bias[:]
+            )
+
+        def inverse(t):
+            inv_1q[t] = work.tile([P, CAPS_OUT], F32, name="inv_1q")
+            nc.scalar.activation(out=inv_1q[t][:], in_=inv_sqrt_1q[t][:], func=ACT.Square)
 
         def unit(t):
             nc.vector.tensor_tensor(
@@ -254,27 +257,33 @@ def tile_capsulenetwork_pb_t_kernel(tc, p, Wr, out):
             return 0 <= t < TILES
 
         for s in range(-AHEAD_TRANSPOSE, TILES):
-            if live(s + AHEAD_TRANSPOSE):
-                transpose_rows(s + AHEAD_TRANSPOSE)
-                group_rows(s + AHEAD_TRANSPOSE)
-            if live(s + AHEAD_MULTIPLY):
-                multiply(s + AHEAD_MULTIPLY, 0)
+            ahead_n, ahead_f, ahead_m = s + AHEAD_NORM, s + AHEAD_FOLD, s + AHEAD_MULTIPLY
+            ahead_q, ahead_t = s + AHEAD_QUANTISE, s + AHEAD_TRANSPOSE
             if live(s):
                 unit(s)
-            if live(s + AHEAD_QUANTISE):
-                quantise_rows(s + AHEAD_QUANTISE)
+            if live(ahead_t):
+                transpose_rows(ahead_t)
+            if live(ahead_q):
+                quantise_rows(ahead_q)
+            if live(ahead_m):
+                multiply(ahead_m, 0)
             if live(s):
                 factor(s)
-            if live(s + AHEAD_FOLD):
-                fold(s + AHEAD_FOLD)
-            if live(s + AHEAD_NORM):
-                length(s + AHEAD_NORM)
-                roots(s + AHEAD_NORM)
-            if live(s + AHEAD_MULTIPLY):
-                square(s + AHEAD_MULTIPLY, 0)
-                multiply(s + AHEAD_MULTIPLY, 1)
-                square(s + AHEAD_MULTIPLY, 1)
+            if live(ahead_n):
+                length(ahead_n)
+                roots(ahead_n)
+            if live(ahead_f):
+                fold(ahead_f)
             if live(s):
                 scale_half(s, 0)
                 scale_half(s, 1)
                 store(s)
+            if live(ahead_t):
+                group_rows(ahead_t)
+            if live(ahead_m):
+                multiply(ahead_m, 1)
+            if live(ahead_n):
+                inverse(ahead_n)
+            if live(ahead_m):
+                square(ahead_m, 0)
+                square(ahead_m, 1)

@@ -23,7 +23,7 @@ PACK = 4
 K_PASS = P * PACK
 PASSES = K // K_PASS
 PLANES = 2
-CAPS_PLANE = CAPS_IN // (PASSES * PLANES)
+CAPS_PASS = CAPS_IN // PASSES
 WORDS_IN = DIM_IN // 2
 COLS_PART = COLS // P
 BANK = 512
@@ -32,15 +32,21 @@ OL_BANK = 2
 OL_HALF = COLS_PART // HALVES
 OH = DIM_OUT // COLS_PART
 TILES = BATCH // P
+OL_SORT = 4
+WEIGHT_LOADS = [16, 16, 16, 12, 4]
 LOAD_WIDTHS = [1, 1, 2] + [4] * 7
+W_BANKS = COLS_PART // OL_BANK
+EARLY_TILES = 1
+WARM_START = 16
+WARM_BETWEEN = 2
 COUPLING = 1.0 / CAPS_OUT
 SQ_EPS = 1e-8
 
 AHEAD_NORM = 1
 AHEAD_FOLD = 2
 AHEAD_MULTIPLY = 3
-AHEAD_QUANTISE = 5
-AHEAD_TRANSPOSE = 7
+AHEAD_QUANTISE = 4
+AHEAD_TRANSPOSE = 5
 
 FLOPS = 2 * BATCH * K * COLS
 
@@ -61,9 +67,12 @@ def tile_capsulenetwork_pb_t_kernel(tc, p, Wr, out):
         ctx.enter_context(tc.manual_schedule())
 
         w_raw = weights.tile([P, CAPS_IN, COLS_PART * DIM_IN], BF16)
-        for plane in range(PASSES * PLANES):
-            caps = slice(plane * CAPS_PLANE, (plane + 1) * CAPS_PLANE)
-            nc.sync.dma_start(out=w_raw[:, caps, :], in_=w_view[:, caps, :])
+        w_loads = []
+        first = 0
+        for width in WEIGHT_LOADS:
+            nc.sync.dma_start(out=w_raw[:, first : first + width, :], in_=w_view[:, first : first + width, :])
+            w_loads.append((first, width))
+            first += width
         p_rows = {}
         first = 0
         for c, width in enumerate(LOAD_WIDTHS):
@@ -83,52 +92,44 @@ def tile_capsulenetwork_pb_t_kernel(tc, p, Wr, out):
         nc.scalar.activation(out=table_warm[:], in_=one_bias[:], func=ACT.Abs_reciprocal_sqrt)
 
         w_raw_words = w_raw[:].bitcast(F32).rearrange("c n (ol w) -> c ol n w", ol=COLS_PART)
-        w_sorted = weights.tile([P, PASSES, COLS_PART, PLANES, P], F32)
+        w_sorted = weights.tile([P, PASSES, COLS_PART, PLANES * P], F32)
+        w_sorted_words = w_sorted[:].rearrange("c g ol (n w) -> c g ol n w", w=WORDS_IN)
         w_grouped = weights.tile([P, PASSES, COLS * PACK], BF16, align_bytes=64)
         w_grouped_words = w_grouped[:].bitcast(F32).rearrange("r g (ol c u) -> r g ol c u", ol=COLS_PART, u=PLANES)
         w_codes = weights.tile([P, PASSES, COLS], U32, align_bytes=64)
         w_scales = weights.tile([P, PASSES, COLS], U8, align_bytes=64)
 
-        def sort_weights(plane):
-            g, q = divmod(plane, PLANES)
-            caps = slice(plane * CAPS_PLANE, (plane + 1) * CAPS_PLANE)
-            for m in range(COLS_PART // OL_BANK):
-                ols = slice(m * OL_BANK, (m + 1) * OL_BANK)
+        def sort_weights(first, width):
+            g, n = divmod(first, CAPS_PASS)
+            for m in range(0, COLS_PART, OL_SORT):
+                ols = slice(m, m + OL_SORT)
                 nc.vector.tensor_copy(
-                    out=w_sorted[:, g, ols, q, :].rearrange("c ol (n w) -> c ol n w", w=WORDS_IN),
-                    in_=w_raw_words[:, ols, caps, :],
+                    out=w_sorted_words[:, g, ols, n : n + width, :], in_=w_raw_words[:, ols, first : first + width, :]
                 )
 
-        def transpose_weights(g):
-            for m in range(COLS_PART // OL_BANK):
-                w_bank = psum.tile([P, OL_BANK, PLANES, P], F32, name="w_bank", tag="bank")
-                for a in range(OL_BANK):
-                    words = w_sorted[:, g, m * OL_BANK + a, :, :].rearrange("c h w -> c (h w)")
-                    for u in range(PLANES):
-                        nc.tensor.transpose(w_bank[:, a, u, :], words[:, u::PLANES], ident[:])
-                nc.scalar.copy(
-                    out=w_grouped_words[:, g, m * OL_BANK : (m + 1) * OL_BANK, :, :],
-                    in_=w_bank[:].rearrange("r a u c -> r a c u"),
-                )
+        def transpose_weights(g, m):
+            w_bank = psum.tile([P, OL_BANK, PLANES, P], F32, name="w_bank", tag="bank")
+            for a in range(OL_BANK):
+                for u in range(PLANES):
+                    nc.tensor.transpose(w_bank[:, a, u, :], w_sorted[:, g, m * OL_BANK + a, u::PLANES], ident[:])
+            nc.scalar.copy(
+                out=w_grouped_words[:, g, m * OL_BANK : (m + 1) * OL_BANK, :, :],
+                in_=w_bank[:].rearrange("r a u c -> r a c u"),
+            )
 
-        def quantise_weights(g):
+        def quantise_weights(g, m):
             width = OL_BANK * P
-            for m in range(COLS_PART // OL_BANK):
-                cols = slice(m * width, (m + 1) * width)
-                nc.vector.quantize_mx(
-                    out=w_codes[:, g, cols].bitcast(FP8X4),
-                    scales=w_scales[:, g, cols],
-                    in_=w_grouped[:, g, m * width * PACK : (m + 1) * width * PACK],
-                )
+            cols = slice(m * width, (m + 1) * width)
+            nc.vector.quantize_mx(
+                out=w_codes[:, g, cols].bitcast(FP8X4),
+                scales=w_scales[:, g, cols],
+                in_=w_grouped[:, g, m * width * PACK : (m + 1) * width * PACK],
+            )
 
-        sort_weights(0)
-        sort_weights(1)
-        transpose_weights(0)
-        sort_weights(2)
-        quantise_weights(0)
-        sort_weights(3)
-        transpose_weights(1)
-        quantise_weights(1)
+        def warm_tensor(count):
+            unread = psum.tile([P, P], F32, name="unread", tag="bank")
+            for x in range(count):
+                nc.tensor.matmul(unread[:], lhsT=ident[:], rhs=ident[:], start=True, stop=True)
 
         flipped = {}
         grouped = {}
@@ -256,14 +257,36 @@ def tile_capsulenetwork_pb_t_kernel(tc, p, Wr, out):
         def live(t):
             return 0 <= t < TILES
 
+        warm_tensor(WARM_START)
+        for first, width in w_loads:
+            if first < CAPS_PASS:
+                sort_weights(first, width)
+        for m in range(W_BANKS):
+            transpose_weights(0, m)
+            warm_tensor(1)
+        for first, width in w_loads:
+            if first >= CAPS_PASS:
+                sort_weights(first, width)
+        warm_tensor(WARM_BETWEEN)
+        for m in range(W_BANKS):
+            quantise_weights(0, m)
+        for m in range(W_BANKS):
+            transpose_weights(1, m)
+            quantise_weights(1, m)
+            if m == W_BANKS // 2 - 1:
+                for t in range(EARLY_TILES):
+                    transpose_rows(t)
+                    group_rows(t)
+                    quantise_rows(t)
+
         for s in range(-AHEAD_TRANSPOSE, TILES):
             ahead_n, ahead_f, ahead_m = s + AHEAD_NORM, s + AHEAD_FOLD, s + AHEAD_MULTIPLY
             ahead_q, ahead_t = s + AHEAD_QUANTISE, s + AHEAD_TRANSPOSE
             if live(s):
                 unit(s)
-            if live(ahead_t):
+            if ahead_t >= EARLY_TILES and live(ahead_t):
                 transpose_rows(ahead_t)
-            if live(ahead_q):
+            if ahead_q >= EARLY_TILES and live(ahead_q):
                 quantise_rows(ahead_q)
             if live(ahead_m):
                 multiply(ahead_m, 0)
@@ -278,7 +301,7 @@ def tile_capsulenetwork_pb_t_kernel(tc, p, Wr, out):
                 scale_half(s, 0)
                 scale_half(s, 1)
                 store(s)
-            if live(ahead_t):
+            if ahead_t >= EARLY_TILES and live(ahead_t):
                 group_rows(ahead_t)
             if live(ahead_m):
                 multiply(ahead_m, 1)

@@ -39,6 +39,7 @@ W_BANKS = COLS_PART // OL_BANK
 EARLY_TILES = 1
 WARM_START = 16
 WARM_BETWEEN = 2
+NUMBERS = 3
 COUPLING = 1.0 / CAPS_OUT
 SQ_EPS = 1e-8
 
@@ -46,7 +47,8 @@ AHEAD_NORM = 1
 AHEAD_FOLD = 2
 AHEAD_MULTIPLY = 3
 AHEAD_QUANTISE = 4
-AHEAD_TRANSPOSE = 5
+AHEAD_TRANSPOSE = 6
+CATCH_UP = 1 - AHEAD_MULTIPLY
 
 FLOPS = 2 * BATCH * K * COLS
 
@@ -62,7 +64,7 @@ def tile_capsulenetwork_pb_t_kernel(tc, p, Wr, out):
         weights = ctx.enter_context(tc.tile_pool(name="weights", bufs=1))
         rows = ctx.enter_context(tc.tile_pool(name="rows", bufs=1))
         work = ctx.enter_context(tc.tile_pool(name="work", bufs=4))
-        sums = ctx.enter_context(tc.tile_pool(name="sums", bufs=2))
+        results = ctx.enter_context(tc.tile_pool(name="results", bufs=16))
         psum = ctx.enter_context(tc.psum_pool(name="psum", bufs=8))
         ctx.enter_context(tc.manual_schedule())
 
@@ -138,10 +140,7 @@ def tile_capsulenetwork_pb_t_kernel(tc, p, Wr, out):
         banks = {}
         squares = {}
         folded = {}
-        lengths = {}
-        inv_roots = {}
-        inv_sqrt_1q = {}
-        inv_1q = {}
+        numbers = {}
         factors = {}
         squashed = {}
 
@@ -193,57 +192,53 @@ def tile_capsulenetwork_pb_t_kernel(tc, p, Wr, out):
             )
 
         def fold(t):
-            folded[t] = sums.tile([P, COLS // 2 + CAPS_OUT], F32, name="folded")
+            folded[t] = work.tile([P, COLS // 2], F32, name="folded")
             for h in range(HALVES):
                 pairs = squares[t][:, h * BANK : (h + 1) * BANK].rearrange(
                     "row (j oh ol) -> row j oh ol", oh=OH, ol=OL_HALF
                 )
                 nc.gpsimd.tensor_tensor(
-                    out=folded[t][:, : COLS // 2].rearrange("row (j h ol) -> row h j ol", h=HALVES, ol=OL_HALF)[:, h],
+                    out=folded[t][:].rearrange("row (j h ol) -> row h j ol", h=HALVES, ol=OL_HALF)[:, h],
                     in0=pairs[:, :, 0, :],
                     in1=pairs[:, :, 1, :],
                     op=ALU.add,
                 )
 
         def length(t):
-            lengths[t] = work.tile([P, CAPS_OUT], F32, name="lengths")
+            numbers[t] = work.tile([P, NUMBERS, CAPS_OUT], F32, name="numbers")
             nc.vector.tensor_reduce(
-                out=lengths[t][:],
-                in_=folded[t][:, : COLS // 2].rearrange("row (j o) -> row j o", j=CAPS_OUT),
+                out=numbers[t][:, 0, :],
+                in_=folded[t][:].rearrange("row (j o) -> row j o", j=CAPS_OUT),
                 axis=mybir.AxisListType.X,
                 op=ALU.add,
             )
 
         def roots(t):
-            inv_roots[t] = work.tile([P, CAPS_OUT], F32, name="inv_roots")
-            inv_sqrt_1q[t] = work.tile([P, CAPS_OUT], F32, name="inv_sqrt_1q")
+            inv_sqrt_1q = work.tile([P, CAPS_OUT], F32, name="inv_sqrt_1q")
             nc.scalar.activation(
-                out=inv_roots[t][:],
-                in_=lengths[t][:],
+                out=inv_sqrt_1q[:], in_=numbers[t][:, 0, :], func=ACT.Abs_reciprocal_sqrt, bias=one_bias[:]
+            )
+            nc.scalar.activation(
+                out=numbers[t][:, 1, :],
+                in_=numbers[t][:, 0, :],
                 func=ACT.Abs_reciprocal_sqrt,
                 bias=eps_bias[:],
                 scale=1.0 / (COUPLING * COUPLING),
             )
-            nc.scalar.activation(
-                out=inv_sqrt_1q[t][:], in_=lengths[t][:], func=ACT.Abs_reciprocal_sqrt, bias=one_bias[:]
-            )
-
-        def inverse(t):
-            inv_1q[t] = work.tile([P, CAPS_OUT], F32, name="inv_1q")
-            nc.scalar.activation(out=inv_1q[t][:], in_=inv_sqrt_1q[t][:], func=ACT.Square)
-
-        def unit(t):
-            nc.vector.tensor_tensor(
-                out=folded[t][:, COLS // 2 :], in0=lengths[t][:], in1=inv_roots[t][:], op=ALU.mult
-            )
+            nc.scalar.activation(out=numbers[t][:, 2, :], in_=inv_sqrt_1q[:], func=ACT.Square)
 
         def factor(t):
             factors[t] = work.tile([P, CAPS_OUT], F32, name="factors")
-            nc.vector.tensor_tensor(out=factors[t][:], in0=folded[t][:, COLS // 2 :], in1=inv_1q[t][:], op=ALU.mult)
+            nc.vector.tensor_reduce(
+                out=factors[t][:],
+                in_=numbers[t][:].rearrange("row x j -> row j x"),
+                axis=mybir.AxisListType.X,
+                op=ALU.mult,
+            )
 
         def scale_half(t, h):
             if h == 0:
-                squashed[t] = work.tile([P, COLS], F32, name="squashed")
+                squashed[t] = results.tile([P, COLS], F32, name="squashed")
             nc.vector.tensor_tensor(
                 out=squashed[t][:].rearrange("row (j oh h ol) -> row h j oh ol", oh=OH, h=HALVES, ol=OL_HALF)[:, h],
                 in0=banks[t, h][:].rearrange("row (ol j oh) -> row j oh ol", ol=OL_HALF, oh=OH),
@@ -281,17 +276,19 @@ def tile_capsulenetwork_pb_t_kernel(tc, p, Wr, out):
 
         for s in range(-AHEAD_TRANSPOSE, TILES):
             ahead_n, ahead_f, ahead_m = s + AHEAD_NORM, s + AHEAD_FOLD, s + AHEAD_MULTIPLY
-            ahead_q, ahead_t = s + AHEAD_QUANTISE, s + AHEAD_TRANSPOSE
-            if live(s):
-                unit(s)
-            if ahead_t >= EARLY_TILES and live(ahead_t):
-                transpose_rows(ahead_t)
+            ahead_q = s + AHEAD_QUANTISE
+            ahead_t = []
+            if s <= CATCH_UP:
+                ahead_t.append(s + AHEAD_TRANSPOSE - 1)
+            if s >= CATCH_UP:
+                ahead_t.append(s + AHEAD_TRANSPOSE)
+            ahead_t = [t for t in ahead_t if t >= EARLY_TILES and live(t)]
+            for t in ahead_t:
+                transpose_rows(t)
             if ahead_q >= EARLY_TILES and live(ahead_q):
                 quantise_rows(ahead_q)
             if live(ahead_m):
                 multiply(ahead_m, 0)
-            if live(s):
-                factor(s)
             if live(ahead_n):
                 length(ahead_n)
                 roots(ahead_n)
@@ -301,12 +298,11 @@ def tile_capsulenetwork_pb_t_kernel(tc, p, Wr, out):
                 scale_half(s, 0)
                 scale_half(s, 1)
                 store(s)
-            if ahead_t >= EARLY_TILES and live(ahead_t):
-                group_rows(ahead_t)
+            if live(ahead_n):
+                factor(ahead_n)
+            for t in ahead_t:
+                group_rows(t)
             if live(ahead_m):
                 multiply(ahead_m, 1)
-            if live(ahead_n):
-                inverse(ahead_n)
-            if live(ahead_m):
                 square(ahead_m, 0)
                 square(ahead_m, 1)

@@ -45,10 +45,11 @@ SQ_EPS = 1e-8
 
 AHEAD_NORM = 1
 AHEAD_FOLD = 2
-AHEAD_MULTIPLY = 3
-AHEAD_QUANTISE = 4
-AHEAD_TRANSPOSE = 6
-CATCH_UP = 1 - AHEAD_MULTIPLY
+AHEAD_SECOND = 3
+AHEAD_FIRST = 4
+AHEAD_QUANTISE = 5
+AHEAD_GROUP = 6
+AHEAD_TRANSPOSE = 7
 
 FLOPS = 2 * BATCH * K * COLS
 
@@ -142,7 +143,6 @@ def tile_capsulenetwork_pb_t_kernel(tc, p, Wr, out):
         folded = {}
         numbers = {}
         factors = {}
-        squashed = {}
 
         def transpose_rows(t):
             words = p_rows[t].bitcast(F32)
@@ -191,18 +191,18 @@ def tile_capsulenetwork_pb_t_kernel(tc, p, Wr, out):
                 scale=COUPLING,
             )
 
-        def fold(t):
-            folded[t] = work.tile([P, COLS // 2], F32, name="folded")
-            for h in range(HALVES):
-                pairs = squares[t][:, h * BANK : (h + 1) * BANK].rearrange(
-                    "row (j oh ol) -> row j oh ol", oh=OH, ol=OL_HALF
-                )
-                nc.gpsimd.tensor_tensor(
-                    out=folded[t][:].rearrange("row (j h ol) -> row h j ol", h=HALVES, ol=OL_HALF)[:, h],
-                    in0=pairs[:, :, 0, :],
-                    in1=pairs[:, :, 1, :],
-                    op=ALU.add,
-                )
+        def fold(t, h):
+            if h == 0:
+                folded[t] = work.tile([P, COLS // 2], F32, name="folded")
+            pairs = squares[t][:, h * BANK : (h + 1) * BANK].rearrange(
+                "row (j oh ol) -> row j oh ol", oh=OH, ol=OL_HALF
+            )
+            nc.gpsimd.tensor_tensor(
+                out=folded[t][:].rearrange("row (j h ol) -> row h j ol", h=HALVES, ol=OL_HALF)[:, h],
+                in0=pairs[:, :, 0, :],
+                in1=pairs[:, :, 1, :],
+                op=ALU.add,
+            )
 
         def length(t):
             numbers[t] = work.tile([P, NUMBERS, CAPS_OUT], F32, name="numbers")
@@ -236,18 +236,23 @@ def tile_capsulenetwork_pb_t_kernel(tc, p, Wr, out):
                 op=ALU.mult,
             )
 
-        def scale_half(t, h):
-            if h == 0:
-                squashed[t] = results.tile([P, COLS], F32, name="squashed")
-            nc.vector.tensor_tensor(
-                out=squashed[t][:].rearrange("row (j oh h ol) -> row h j oh ol", oh=OH, h=HALVES, ol=OL_HALF)[:, h],
-                in0=banks[t, h][:].rearrange("row (ol j oh) -> row j oh ol", ol=OL_HALF, oh=OH),
-                in1=factors[t][:].unsqueeze(2).unsqueeze(3).to_broadcast([P, CAPS_OUT, OH, OL_HALF]),
-                op=ALU.mult,
-            )
-
-        def store(t):
-            nc.sync.dma_start(out=out_view[:, t, :], in_=squashed[t][:])
+        def finish(t):
+            squashed = results.tile([P, CAPS_OUT, DIM_OUT], F32, name="squashed")
+            pieces = 2 if t == TILES - 1 else 1
+            width = CAPS_OUT // pieces
+            for x in range(pieces):
+                caps = slice(x * width, (x + 1) * width)
+                for h in range(HALVES):
+                    nc.vector.tensor_tensor(
+                        out=squashed[:].rearrange("row j (oh h ol) -> row h j oh ol", oh=OH, h=HALVES)[:, h, caps],
+                        in0=banks[t, h][:].rearrange("row (ol j oh) -> row j oh ol", ol=OL_HALF, oh=OH)[:, caps],
+                        in1=factors[t][:, caps].unsqueeze(2).unsqueeze(3).to_broadcast([P, width, OH, OL_HALF]),
+                        op=ALU.mult,
+                    )
+                nc.sync.dma_start(
+                    out=out_view[:, t, x * width * DIM_OUT : (x + 1) * width * DIM_OUT],
+                    in_=squashed[:, caps, :].rearrange("row j o -> row (j o)"),
+                )
 
         def live(t):
             return 0 <= t < TILES
@@ -275,34 +280,29 @@ def tile_capsulenetwork_pb_t_kernel(tc, p, Wr, out):
                     quantise_rows(t)
 
         for s in range(-AHEAD_TRANSPOSE, TILES):
-            ahead_n, ahead_f, ahead_m = s + AHEAD_NORM, s + AHEAD_FOLD, s + AHEAD_MULTIPLY
-            ahead_q = s + AHEAD_QUANTISE
-            ahead_t = []
-            if s <= CATCH_UP:
-                ahead_t.append(s + AHEAD_TRANSPOSE - 1)
-            if s >= CATCH_UP:
-                ahead_t.append(s + AHEAD_TRANSPOSE)
-            ahead_t = [t for t in ahead_t if t >= EARLY_TILES and live(t)]
-            for t in ahead_t:
-                transpose_rows(t)
-            if ahead_q >= EARLY_TILES and live(ahead_q):
-                quantise_rows(ahead_q)
-            if live(ahead_m):
-                multiply(ahead_m, 0)
-            if live(ahead_n):
-                length(ahead_n)
-                roots(ahead_n)
-            if live(ahead_f):
-                fold(ahead_f)
+            if live(s + AHEAD_NORM):
+                length(s + AHEAD_NORM)
             if live(s):
-                scale_half(s, 0)
-                scale_half(s, 1)
-                store(s)
-            if live(ahead_n):
-                factor(ahead_n)
-            for t in ahead_t:
-                group_rows(t)
-            if live(ahead_m):
-                multiply(ahead_m, 1)
-                square(ahead_m, 0)
-                square(ahead_m, 1)
+                finish(s)
+            if live(s + AHEAD_SECOND):
+                multiply(s + AHEAD_SECOND, 1)
+            if live(s + AHEAD_FOLD):
+                square(s + AHEAD_FOLD, 1)
+            if live(s + AHEAD_NORM):
+                roots(s + AHEAD_NORM)
+            if live(s + AHEAD_SECOND):
+                square(s + AHEAD_SECOND, 0)
+            if s + AHEAD_GROUP >= EARLY_TILES and live(s + AHEAD_GROUP):
+                group_rows(s + AHEAD_GROUP)
+            if live(s + AHEAD_NORM):
+                factor(s + AHEAD_NORM)
+            if live(s + AHEAD_FOLD):
+                fold(s + AHEAD_FOLD, 1)
+            if live(s + AHEAD_FIRST):
+                multiply(s + AHEAD_FIRST, 0)
+            if s + AHEAD_TRANSPOSE >= EARLY_TILES and live(s + AHEAD_TRANSPOSE):
+                transpose_rows(s + AHEAD_TRANSPOSE)
+            if s + AHEAD_QUANTISE >= EARLY_TILES and live(s + AHEAD_QUANTISE):
+                quantise_rows(s + AHEAD_QUANTISE)
+            if live(s + AHEAD_SECOND):
+                fold(s + AHEAD_SECOND, 0)

from contextlib import ExitStack

import concourse.mybir as mybir
from concourse.masks import make_identity

F32 = mybir.dt.float32
BF16 = mybir.dt.bfloat16
U32 = mybir.dt.uint32
U8 = mybir.dt.uint8
FP8X4 = mybir.dt.float8_e4m3fn_x4
ACT = mybir.ActivationFunctionType
ALU = mybir.AluOpType

P = 128
BATCH = 4096
CAPS_IN = 64
DIM_IN = 16
CAPS_OUT = 64
DIM_OUT = 16
K = CAPS_IN * DIM_IN
COLS = CAPS_OUT * DIM_OUT
PACK = 4
K_PASS = P * PACK
PASSES = K // K_PASS
PLANES = 2
CAPS_PASS = CAPS_IN // PASSES
WORDS_IN = DIM_IN // 2
COLS_PART = COLS // P
BANK = 512
HALVES = COLS // BANK
OL_BANK = 2
OL_HALF = COLS_PART // HALVES
OH = DIM_OUT // COLS_PART
TILES = BATCH // P
OL_SORT = 4
WEIGHT_LOADS = [16, 16, 16, 12, 4]
LOAD_WIDTHS = [1, 1, 2] + [4] * 7
W_BANKS = COLS_PART // OL_BANK
EARLY_TILES = 1
WARM_START = 16
WARM_BETWEEN = 2
NUMBERS = 3
COUPLING = 1.0 / CAPS_OUT
SQ_EPS = 1e-8

AHEAD_NORM = 1
AHEAD_FOLD = 2
AHEAD_SECOND = 3
AHEAD_FIRST = 4
AHEAD_QUANTISE = 5
AHEAD_GROUP = 6
AHEAD_TRANSPOSE = 7

FLOPS = 2 * BATCH * K * COLS


def tile_capsulenetwork_pb_t_kernel(tc, p, Wr, out):
    nc = tc.nc
    p_view = p.rearrange("(row t) n i -> row t (n i)", t=TILES)
    out_view = out.rearrange("(row t) j o -> row t (j o)", t=TILES)
    w_view = Wr.rearrange("n j (oh ol) i -> (j oh) n (ol i)", ol=COLS_PART)

    with ExitStack() as ctx:
        const = ctx.enter_context(tc.tile_pool(name="const", bufs=1))
        weights = ctx.enter_context(tc.tile_pool(name="weights", bufs=1))
        rows = ctx.enter_context(tc.tile_pool(name="rows", bufs=1))
        work = ctx.enter_context(tc.tile_pool(name="work", bufs=4))
        results = ctx.enter_context(tc.tile_pool(name="results", bufs=16))
        psum = ctx.enter_context(tc.psum_pool(name="psum", bufs=8))
        ctx.enter_context(tc.manual_schedule())

        w_raw = weights.tile([P, CAPS_IN, COLS_PART * DIM_IN], BF16)
        w_loads = []
        first = 0
        for width in WEIGHT_LOADS:
            nc.sync.dma_start(out=w_raw[:, first : first + width, :], in_=w_view[:, first : first + width, :])
            w_loads.append((first, width))
            first += width
        p_rows = {}
        first = 0
        for c, width in enumerate(LOAD_WIDTHS):
            chunk = rows.tile([P, width, K], BF16, name="p_rows%d" % c)
            nc.sync.dma_start(out=chunk[:], in_=p_view[:, first : first + width, :])
            for x in range(width):
                p_rows[first + x] = chunk[:, x, :]
            first += width

        ident = const.tile([P, P], F32)
        make_identity(nc, ident[:])
        eps_bias = const.tile([P, 1], F32)
        nc.vector.memset(eps_bias[:], SQ_EPS / (COUPLING * COUPLING))
        one_bias = const.tile([P, 1], F32)
        nc.vector.memset(one_bias[:], 1.0)
        table_warm = const.tile([P, 1], F32)
        nc.scalar.activation(out=table_warm[:], in_=one_bias[:], func=ACT.Abs_reciprocal_sqrt)

        w_raw_words = w_raw[:].bitcast(F32).rearrange("c n (ol w) -> c ol n w", ol=COLS_PART)
        w_sorted = weights.tile([P, PASSES, COLS_PART, PLANES * P], F32)
        w_sorted_words = w_sorted[:].rearrange("c g ol (n w) -> c g ol n w", w=WORDS_IN)
        w_grouped = weights.tile([P, PASSES, COLS * PACK], BF16, align_bytes=64)
        w_grouped_words = w_grouped[:].bitcast(F32).rearrange("r g (ol c u) -> r g ol c u", ol=COLS_PART, u=PLANES)
        w_codes = weights.tile([P, PASSES, COLS], U32, align_bytes=64)
        w_scales = weights.tile([P, PASSES, COLS], U8, align_bytes=64)

        def sort_weights(first, width):
            g, n = divmod(first, CAPS_PASS)
            for m in range(0, COLS_PART, OL_SORT):
                ols = slice(m, m + OL_SORT)
                nc.vector.tensor_copy(
                    out=w_sorted_words[:, g, ols, n : n + width, :], in_=w_raw_words[:, ols, first : first + width, :]
                )

        def transpose_weights(g, m):
            w_bank = psum.tile([P, OL_BANK, PLANES, P], F32, name="w_bank", tag="bank")
            for a in range(OL_BANK):
                for u in range(PLANES):
                    nc.tensor.transpose(w_bank[:, a, u, :], w_sorted[:, g, m * OL_BANK + a, u::PLANES], ident[:])
            nc.scalar.copy(
                out=w_grouped_words[:, g, m * OL_BANK : (m + 1) * OL_BANK, :, :],
                in_=w_bank[:].rearrange("r a u c -> r a c u"),
            )

        def quantise_weights(g, m):
            width = OL_BANK * P
            cols = slice(m * width, (m + 1) * width)
            nc.vector.quantize_mx(
                out=w_codes[:, g, cols].bitcast(FP8X4),
                scales=w_scales[:, g, cols],
                in_=w_grouped[:, g, m * width * PACK : (m + 1) * width * PACK],
            )

        def warm_tensor(count):
            unread = psum.tile([P, P], F32, name="unread", tag="bank")
            for x in range(count):
                nc.tensor.matmul(unread[:], lhsT=ident[:], rhs=ident[:], start=True, stop=True)

        flipped = {}
        grouped = {}
        codes = {}
        scales = {}
        banks = {}
        squares = {}
        folded = {}
        numbers = {}
        factors = {}

        def transpose_rows(t):
            words = p_rows[t].bitcast(F32)
            flipped[t] = psum.tile([P, PASSES * PLANES, P], F32, name="flipped", tag="bank")
            for x in range(PASSES * PLANES):
                nc.tensor.transpose(flipped[t][:, x, :], words[:, (x // PLANES) * PLANES * P + x % PLANES : (x // PLANES + 1) * PLANES * P : PLANES], ident[:])

        def group_rows(t):
            grouped[t] = work.tile([P, PASSES, P * PACK], BF16, name="grouped", align_bytes=64)
            nc.scalar.copy(
                out=grouped[t][:].bitcast(F32).rearrange("r g (row u) -> r g row u", u=PLANES),
                in_=flipped[t][:].rearrange("r (g u) row -> r g row u", u=PLANES),
            )

        def quantise_rows(t):
            codes[t] = work.tile([P, PASSES, P], U32, name="codes", align_bytes=64)
            scales[t] = work.tile([P, PASSES, P], U8, name="scales", align_bytes=64)
            nc.vector.quantize_mx(
                out=codes[t][:].rearrange("r g row -> r (g row)").bitcast(FP8X4),
                scales=scales[t][:].rearrange("r g row -> r (g row)"),
                in_=grouped[t][:].rearrange("r g c -> r (g c)"),
            )

        def multiply(t, h):
            cols = slice(h * BANK, (h + 1) * BANK)
            bank = psum.tile([P, BANK], F32, tag="bank")
            for g in range(PASSES):
                nc.tensor.matmul_mx(
                    out=bank[:],
                    lhsT=codes[t][:, g, :].bitcast(FP8X4),
                    lhsT_scale=scales[t][:, g, :],
                    rhs=w_codes[:, g, cols].bitcast(FP8X4),
                    rhs_scale=w_scales[:, g, cols],
                    start=(g == 0),
                    stop=(g == PASSES - 1),
                )
            banks[t, h] = bank

        def square(t, h):
            if h == 0:
                squares[t] = work.tile([P, COLS], F32, name="squares")
            nc.scalar.activation(
                out=squares[t][:, h * BANK : (h + 1) * BANK].rearrange("row (c ol) -> row c ol", ol=OL_HALF),
                in_=banks[t, h][:].rearrange("row (ol c) -> row c ol", ol=OL_HALF),
                func=ACT.Square,
                scale=COUPLING,
            )

        def fold(t, h):
            if h == 0:
                folded[t] = work.tile([P, COLS // 2], F32, name="folded")
            pairs = squares[t][:, h * BANK : (h + 1) * BANK].rearrange(
                "row (j oh ol) -> row j oh ol", oh=OH, ol=OL_HALF
            )
            nc.gpsimd.tensor_tensor(
                out=folded[t][:].rearrange("row (j h ol) -> row h j ol", h=HALVES, ol=OL_HALF)[:, h],
                in0=pairs[:, :, 0, :],
                in1=pairs[:, :, 1, :],
                op=ALU.add,
            )

        def length(t):
            numbers[t] = work.tile([P, NUMBERS, CAPS_OUT], F32, name="numbers")
            nc.vector.tensor_reduce(
                out=numbers[t][:, 0, :],
                in_=folded[t][:].rearrange("row (j o) -> row j o", j=CAPS_OUT),
                axis=mybir.AxisListType.X,
                op=ALU.add,
            )

        def roots(t):
            inv_sqrt_1q = work.tile([P, CAPS_OUT], F32, name="inv_sqrt_1q")
            nc.scalar.activation(
                out=inv_sqrt_1q[:], in_=numbers[t][:, 0, :], func=ACT.Abs_reciprocal_sqrt, bias=one_bias[:]
            )
            nc.scalar.activation(
                out=numbers[t][:, 1, :],
                in_=numbers[t][:, 0, :],
                func=ACT.Abs_reciprocal_sqrt,
                bias=eps_bias[:],
                scale=1.0 / (COUPLING * COUPLING),
            )
            nc.scalar.activation(out=numbers[t][:, 2, :], in_=inv_sqrt_1q[:], func=ACT.Square)

        def factor(t):
            factors[t] = work.tile([P, CAPS_OUT], F32, name="factors")
            nc.vector.tensor_reduce(
                out=factors[t][:],
                in_=numbers[t][:].rearrange("row x j -> row j x"),
                axis=mybir.AxisListType.X,
                op=ALU.mult,
            )

        def finish(t):
            squashed = results.tile([P, CAPS_OUT, DIM_OUT], F32, name="squashed")
            pieces = 2 if t == TILES - 1 else 1
            width = CAPS_OUT // pieces
            for x in range(pieces):
                caps = slice(x * width, (x + 1) * width)
                for h in range(HALVES):
                    nc.vector.tensor_tensor(
                        out=squashed[:].rearrange("row j (oh h ol) -> row h j oh ol", oh=OH, h=HALVES)[:, h, caps],
                        in0=banks[t, h][:].rearrange("row (ol j oh) -> row j oh ol", ol=OL_HALF, oh=OH)[:, caps],
                        in1=factors[t][:, caps].unsqueeze(2).unsqueeze(3).to_broadcast([P, width, OH, OL_HALF]),
                        op=ALU.mult,
                    )
                nc.sync.dma_start(
                    out=out_view[:, t, x * width * DIM_OUT : (x + 1) * width * DIM_OUT],
                    in_=squashed[:, caps, :].rearrange("row j o -> row (j o)"),
                )

        def live(t):
            return 0 <= t < TILES

        warm_tensor(WARM_START)
        for first, width in w_loads:
            if first < CAPS_PASS:
                sort_weights(first, width)
        for m in range(W_BANKS):
            transpose_weights(0, m)
            warm_tensor(1)
        for first, width in w_loads:
            if first >= CAPS_PASS:
                sort_weights(first, width)
        warm_tensor(WARM_BETWEEN)
        for m in range(W_BANKS):
            quantise_weights(0, m)
        for m in range(W_BANKS):
            transpose_weights(1, m)
            quantise_weights(1, m)
            if m == W_BANKS // 2 - 1:
                for t in range(EARLY_TILES):
                    transpose_rows(t)
                    group_rows(t)
                    quantise_rows(t)

        for s in range(-AHEAD_TRANSPOSE, TILES):
            if live(s + AHEAD_NORM):
                length(s + AHEAD_NORM)
            if live(s):
                finish(s)
            if live(s + AHEAD_SECOND):
                multiply(s + AHEAD_SECOND, 1)
            if live(s + AHEAD_FOLD):
                square(s + AHEAD_FOLD, 1)
            if live(s + AHEAD_NORM):
                roots(s + AHEAD_NORM)
            if live(s + AHEAD_SECOND):
                square(s + AHEAD_SECOND, 0)
            if s + AHEAD_GROUP >= EARLY_TILES and live(s + AHEAD_GROUP):
                group_rows(s + AHEAD_GROUP)
            if live(s + AHEAD_NORM):
                factor(s + AHEAD_NORM)
            if live(s + AHEAD_FOLD):
                fold(s + AHEAD_FOLD, 1)
            if live(s + AHEAD_FIRST):
                multiply(s + AHEAD_FIRST, 0)
            if s + AHEAD_TRANSPOSE >= EARLY_TILES and live(s + AHEAD_TRANSPOSE):
                transpose_rows(s + AHEAD_TRANSPOSE)
            if s + AHEAD_QUANTISE >= EARLY_TILES and live(s + AHEAD_QUANTISE):
                quantise_rows(s + AHEAD_QUANTISE)
            if live(s + AHEAD_SECOND):
                fold(s + AHEAD_SECOND, 0)
